import numpy as np
import ml_dtypes


def mxq(x, axis, fmt="e4m3"):
    dtype, down = {"e4m3": (ml_dtypes.float8_e4m3fn, 7), "e5m2": (ml_dtypes.float8_e5m2, 14)}[fmt]
    v = np.moveaxis(np.asarray(x, np.float32).astype(ml_dtypes.bfloat16).astype(np.float64), axis, -1)
    blocks = v.reshape(v.shape[:-1] + (-1, 32))
    amax = np.abs(blocks).max(-1, keepdims=True)
    byte = np.maximum(np.where(amax > 0, np.frexp(amax)[1] - 1 + 127, 0) - down, 1)
    scale = np.exp2(byte - 127.0)
    codes = (blocks / scale).astype(np.float32).astype(dtype).astype(np.float64)
    return np.moveaxis((codes * scale).reshape(v.shape), -1, axis)


WIDE = False


def mx_kscale(k):
    if not WIDE:
        return np.ones(k)
    levels = np.array([10, -10, 5, -5, 0])
    if k % 512:
        return np.exp2(np.random.permutation(np.resize(levels, k // 32))).repeat(32)
    a = np.empty((k // 512, 16))
    for p in range(k // 512):
        a[p, :8] = np.random.permutation(np.resize(levels, 8))
        for g in range(8):
            far = levels[np.abs(levels - a[p, g]) >= 10]
            a[p, g + 8] = far[np.random.randint(len(far))]
    return np.exp2(a.ravel()).repeat(32)


BF16 = ml_dtypes.bfloat16


def bf(x):
    return np.asarray(x, np.float32).astype(BF16)


def f64(x):
    return np.asarray(x).astype(np.float64)


B, S, D, E, R = 2, 1024, 4096, 8, 64


def draw0():
    s = mx_kscale(D)
    return {"x": bf(np.random.standard_normal((B, S, D)) * s),
            "W": bf(np.random.standard_normal((E, R, D)) * (1.0 / np.sqrt(D)) / s)}


def core(x, W):
    xq = mxq(f64(x), 2, "e4m3")
    Wq = mxq(f64(W), 2, "e4m3")
    y = xq[None, :, :, :] @ Wq.transpose(0, 2, 1)[:, None, :, :]
    return tuple(y[e] for e in range(W.shape[0]))


def e4m3fn_bytes(y):
    return np.clip(np.asarray(y, np.float64), -448.0, 448.0).astype(np.float32).astype(ml_dtypes.float8_e4m3fn).view(np.uint8)


def e4m3fn_values(b):
    return np.asarray(b, np.uint8).view(ml_dtypes.float8_e4m3fn).astype(np.float64)


def setup_inputs():
    d = draw0()
    x0 = np.asarray(d['x']).astype(np.float64)
    s = (np.max(np.abs(x0), axis=(0, 1), keepdims=True) / 448.0).astype(np.float32)
    out = {}
    for k, v in d.items():
        if k == 'x':
            out['x_bytes'] = e4m3fn_bytes(x0 / s.astype(np.float64))
            out['x_scale'] = s
        else:
            out[k] = v
    return out


def reference(x_bytes, x_scale, W):
    return core(e4m3fn_values(x_bytes) * x_scale.astype(np.float64), W)

@@ -1,0 +1,299 @@
+from contextlib import ExitStack
+
+import concourse.mybir as mybir
+from concourse.masks import make_identity
+
+FLOPS = 2 * 2048 * 4096 * 512
+
+F32 = mybir.dt.float32
+BF16 = mybir.dt.bfloat16
+U32 = mybir.dt.uint32
+U8 = mybir.dt.uint8
+FP8 = mybir.dt.float8_e4m3fn
+FP8X4 = mybir.dt.float8_e4m3fn_x4
+MULT = mybir.AluOpType.mult
+COPY = mybir.ActivationFunctionType.Copy
+
+P = 128
+K = 4096
+NT = 16
+NE = 8
+R = 64
+NW = NE * R
+PASSES = 8
+CH = 1024
+GROUPS = ((0, 4), (4, 8), (8, 12), (12, 15), (15, 16))
+XT = (4, 5, 6, 7, 8, 10, 11, 12, 13, 14)
+
+
+def tile_moelineara_kernel(tc, x_bytes, x_scale, W, *outs):
+    nc = tc.nc
+    xv = x_bytes.flatten_outer_dims().rearrange("(p j) k -> p j k", j=NT)
+    sv = x_scale.rearrange("a b k -> (a b k)")
+    wv = W.flatten_outer_dims().rearrange("(i p) k -> p i k", p=P)
+    ov = [o.flatten_outer_dims().rearrange("(p j) r -> p j r", j=NT) for o in outs]
+
+    with ExitStack() as ctx:
+        const = ctx.enter_context(tc.tile_pool(name="const", bufs=1))
+        xb_pool = ctx.enter_context(tc.tile_pool(name="xbp", bufs=NT))
+        xp_pool = ctx.enter_context(tc.tile_pool(name="xpp", bufs=3))
+        grp_pool = ctx.enter_context(tc.tile_pool(name="grpp", bufs=8))
+        xc_pool = ctx.enter_context(tc.tile_pool(name="xcp", bufs=4))
+        xq_pool = ctx.enter_context(tc.tile_pool(name="xqp", bufs=3))
+        res_pool = ctx.enter_context(tc.tile_pool(name="resp", bufs=2))
+        tp_pool = ctx.enter_context(tc.psum_pool(name="tpp", bufs=6))
+        acc_pool = ctx.enter_context(tc.psum_pool(name="accp", bufs=2))
+
+        ident = const.tile([P, P], F32, name="ident")
+        make_identity(nc, ident[:])
+        warm = const.tile([P, 1], F32, name="warm")
+        nc.scalar.copy(out=warm[:], in_=ident[:, 0:1])
+
+        sc = [const.tile([P, CH], F32, name="sc%d" % c) for c in range(K // CH)]
+        wraw = [const.tile([P, 4, CH], BF16, name="wraw%d" % c) for c in range(K // CH)]
+        wc = [const.tile([P, NW], U32, name="wc%d" % g, align_bytes=64) for g in range(PASSES)]
+        ws = [const.tile([P, NW], U8, name="ws%d" % g, align_bytes=64) for g in range(PASSES)]
+        sk = const.tile([P, 4], F32, name="sk")
+        xq = {}
+        tpx = {}
+        planes = {}
+        xb = {}
+        xp = {}
+        grp = {}
+        xc = {}
+        xs = {}
+        acc = {}
+        res = {}
+
+        def load_scale(c):
+            nc.sync.dma_start(out=sc[c][:], in_=sv[c * CH : (c + 1) * CH].partition_broadcast(P))
+
+        def load_x(j, c0=0, c1=K):
+            if j not in xb:
+                xb[j] = xb_pool.tile([P, K], U8, name="xb")
+            nc.sync.dma_start(out=xb[j][:, c0:c1], in_=xv[:, j, c0:c1])
+
+        def load_w(c):
+            nc.sync.dma_start(out=wraw[c][:], in_=wv[:, :, c * CH : (c + 1) * CH])
+
+        def product(j, c):
+            if j not in xp:
+                xp[j] = xp_pool.tile([P, K], BF16, name="xp")
+            width = 512 if (c == 3 and j in XT) else CH
+            cols = slice(c * CH, c * CH + width)
+            nc.vector.tensor_tensor(
+                out=xp[j][:, cols], in0=xb[j][:, cols].bitcast(FP8), in1=sc[c][:, 0:width], op=MULT
+            )
+
+        def widen(j):
+            if j in XT:
+                xq[j] = xq_pool.tile([P, 512], BF16, name="xq")
+                nc.scalar.copy(out=xq[j][:], in_=xb[j][:, K - 512 : K].bitcast(FP8))
+
+        def scaled_turn(j):
+            if j not in XT:
+                return
+            grp[("x", j, 1)] = grp_pool.tile([P, 2048], BF16, name="grp", align_bytes=64)
+            qwords = xq[j][:].bitcast(F32)
+            tpx[j] = tp_pool.tile([P, 2, 2, P], F32, name="tp")
+            for u in range(2):
+                nc.tensor.transpose(tpx[j][:, 0, u, :], qwords[:, u:256:2], ident[:])
+
+        def scaled_out(j, u):
+            if j not in XT:
+                return
+            if u == 0:
+                planes[j] = xq_pool.tile([P, 4, P], BF16, name="planes")
+            pair = tpx[j][:, 0, u, :].bitcast(BF16).rearrange("p (r e) -> p r e", e=2)
+            for e in range(2):
+                t = 2 * u + e
+                nc.scalar.activation(
+                    out=planes[j][:, t, :], in_=pair[:, :, e], func=COPY, scale=sk[:, t : t + 1]
+                )
+            if u == 1:
+                nc.scalar.copy(
+                    out=grp[("x", j, 1)][:, 1536:2048].rearrange("p (r t) -> p r t", t=4),
+                    in_=planes[j][:].rearrange("p t r -> p r t"),
+                )
+
+        def turn_last(j):
+            gw = grp[("x", j, 1)][:].bitcast(F32)
+            words = xp[j][:].bitcast(F32)
+            tp = tp_pool.tile([P, 2, 2, P], F32, name="tp")
+            for u in range(2):
+                nc.tensor.transpose(tp[:, 0, u, :], words[:, 256 * 6 + u : 256 * 7 : 2], ident[:])
+            nc.scalar.copy(
+                out=gw[:, 512:768].rearrange("p (r u) -> p r u", u=2),
+                in_=tp[:, 0, :, :].rearrange("p u r -> p r u"),
+            )
+
+        def bank(key, b, slices):
+            if key not in grp:
+                grp[key] = grp_pool.tile([P, 2048], BF16, name="grp", align_bytes=64)
+            gw = grp[key][:].bitcast(F32)
+            tp = tp_pool.tile([P, 2, 2, P], F32, name="tp")
+            for a in range(2):
+                for u in range(2):
+                    nc.tensor.transpose(tp[:, a, u, :], slices[a][u], ident[:])
+            nc.scalar.copy(
+                out=gw[:, 512 * b : 512 * (b + 1)].rearrange("p (a r u) -> p a r u", a=2, u=2),
+                in_=tp[:].rearrange("p a u r -> p a r u"),
+            )
+
+        def turn_x(j, h, b):
+            if h == 1 and b == 1 and j in XT:
+                turn_last(j)
+                return
+            words = xp[j][:].bitcast(F32)
+            bank(
+                ("x", j, h),
+                b,
+                [
+                    [words[:, 256 * g + u : 256 * (g + 1) : 2] for u in range(2)]
+                    for g in (4 * h + 2 * b, 4 * h + 2 * b + 1)
+                ],
+            )
+
+        def half(j, h):
+            if h == 0:
+                scaled_turn(j)
+                scaled_out(j, 0)
+            else:
+                scaled_out(j, 1)
+                widen(j + 1)
+            for b in range(2):
+                product(j, 2 * h + b)
+            for b in range(2):
+                turn_x(j, h, b)
+
+        def turn_w(g):
+            words = wraw[g // 2][:].rearrange("p i k -> p (i k)").bitcast(F32)
+            gl = g % 2
+            for b in range(2):
+                bank(
+                    ("w", g),
+                    b,
+                    [
+                        [
+                            words[:, 512 * i + 256 * gl + u : 512 * i + 256 * (gl + 1) : 2]
+                            for u in range(2)
+                        ]
+                        for i in (2 * b, 2 * b + 1)
+                    ],
+                )
+
+        def quant_x(j, h, b0=0, b1=2):
+            if j not in xc:
+                xc[j] = xc_pool.tile([P, 1024], U32, name="xc", align_bytes=64)
+                xs[j] = xc_pool.tile([P, 1024], U8, name="xs", align_bytes=64)
+            cols = slice(512 * h + 256 * b0, 512 * h + 256 * b1)
+            nc.vector.quantize_mx(
+                out=xc[j][:, cols].bitcast(FP8X4),
+                scales=xs[j][:, cols],
+                in_=grp[("x", j, h)][:, 1024 * b0 : 1024 * b1],
+            )
+
+        def quant_w(g):
+            nc.vector.quantize_mx(out=wc[g][:].bitcast(FP8X4), scales=ws[g][:], in_=grp[("w", g)][:])
+
+        def finish(j):
+            for j0, j1 in GROUPS:
+                if j0 <= j < j1:
+                    if j == j0:
+                        res[j0] = res_pool.tile([P, NE, j1 - j0, R], F32, name="res")
+                    nc.scalar.copy(
+                        out=res[j0][:, :, j - j0, :],
+                        in_=acc[j][:].rearrange("p (e r) -> p e r", e=NE),
+                    )
+                    if j == j1 - 1:
+                        for e in range(NE):
+                            nc.sync.dma_start(out=ov[e][:, j0:j1, :], in_=res[j0][:, e, :, :])
+
+        def passes(j, g0, g1):
+            if g0 == 0:
+                acc[j] = acc_pool.tile([P, NW], F32, name="acc")
+            for g in range(g0, g1):
+                cols = slice(P * g, P * (g + 1))
+                nc.tensor.matmul_mx(
+                    out=acc[j][:],
+                    lhsT=xc[j][:, cols].bitcast(FP8X4),
+                    lhsT_scale=xs[j][:, cols],
+                    rhs=wc[g][:].bitcast(FP8X4),
+                    rhs_scale=ws[g][:],
+                    start=(g == 0),
+                    stop=(g == PASSES - 1),
+                )
+            if g1 == PASSES:
+                finish(j)
+
+        with tc.manual_schedule():
+            load_scale(0)
+            load_x(0, 0, 2048)
+            nc.sync.dma_start(out=sk[:], in_=sv[K - 512 : K].rearrange("(p t) -> p t", t=4))
+            load_scale(1)
+            load_x(0, 2048, K)
+            load_scale(2)
+            load_scale(3)
+            load_x(1)
+            load_w(0)
+            load_w(1)
+            load_x(2)
+            load_w(2)
+            load_w(3)
+            for j in range(3, NT):
+                load_x(j)
+
+            widen(0)
+            for j in (0, 1):
+                half(j, 0)
+                half(j, 1)
+            for j in (0, 1):
+                quant_x(j, 0)
+                quant_x(j, 1)
+            for g in range(4):
+                turn_w(g)
+            half(2, 0)
+            half(2, 1)
+            for g in range(4):
+                quant_w(g)
+            for g in range(4, 8):
+                turn_w(g)
+            passes(0, 0, 4)
+            passes(1, 0, 4)
+            half(3, 0)
+            half(3, 1)
+            quant_x(2, 0)
+            quant_x(2, 1)
+            for g in range(4, 8):
+                quant_w(g)
+            passes(0, 4, 8)
+            passes(1, 4, 8)
+            passes(2, 0, 8)
+            for j in range(3, 14):
+                for h in range(2):
+                    half(j + 1, h)
+                    quant_x(j, h)
+                    passes(j, 4 * h, 4 * h + 4)
+            scaled_turn(15)
+            scaled_out(15, 0)
+            quant_x(14, 0)
+            passes(14, 0, 4)
+            product(15, 0)
+            turn_x(15, 0, 0)
+            scaled_out(15, 1)
+            quant_x(14, 1)
+            passes(14, 4, 8)
+            product(15, 1)
+            turn_x(15, 0, 1)
+            product(15, 2)
+            turn_x(15, 1, 0)
+            quant_x(15, 0, 0, 1)
+            passes(15, 0, 2)
+            product(15, 3)
+            turn_x(15, 1, 1)
+            quant_x(15, 0, 1, 2)
+            passes(15, 2, 4)
+            quant_x(15, 1, 0, 1)
+            passes(15, 4, 6)
+            quant_x(15, 1, 1, 2)
+            passes(15, 6, 8)

@@ -54,6 +54,8 @@ def tile_moelineara_kernel(tc, x_bytes, x_scale, W, *outs):
         wc = [const.tile([P, NW], U32, name="wc%d" % g, align_bytes=64) for g in range(PASSES)]
         ws = [const.tile([P, NW], U8, name="ws%d" % g, align_bytes=64) for g in range(PASSES)]
         sk = const.tile([P, 4], F32, name="sk")
+        srow = const.tile([P, P], F32, name="srow")
+        scol = const.tile([P, K // P], F32, name="scol")
         xq = {}
         tpx = {}
         planes = {}
@@ -65,8 +67,25 @@ def tile_moelineara_kernel(tc, x_bytes, x_scale, W, *outs):
         acc = {}
         res = {}
 
-        def load_scale(c):
-            nc.sync.dma_start(out=sc[c][:], in_=sv[c * CH : (c + 1) * CH].partition_broadcast(P))
+        def load_scale():
+            nc.vector.memset(srow[32:64, :], 0.0)
+            nc.vector.memset(srow[64:128, :], 0.0)
+            nc.sync.dma_start(out=srow[0:32, :], in_=sv.rearrange("(m r) -> m r", r=P))
+
+        def turn_scale():
+            tp = tp_pool.tile([P, 2, 2, P], F32, name="tp")
+            nc.tensor.transpose(tp[:, 0, 0, :], srow[:], ident[:])
+            nc.scalar.copy(out=scol[:], in_=tp[:, 0, 0, 0 : K // P])
+
+        def spread_scale(b):
+            tp = tp_pool.tile([P, 2, 2, P], F32, name="tp")
+            for i in range(4):
+                m = 4 * b + i
+                nc.tensor.transpose(tp[:, i // 2, i % 2, :], scol[:, m : m + 1].to_broadcast([P, P]), ident[:])
+            nc.scalar.copy(
+                out=sc[b // 2][:, 512 * (b % 2) : 512 * (b % 2 + 1)],
+                in_=tp[:].rearrange("p a u r -> p (a u r)"),
+            )
 
         def load_x(j, c0=0, c1=K):
             if j not in xb:
@@ -83,6 +102,17 @@ def tile_moelineara_kernel(tc, x_bytes, x_scale, W, *outs):
             cols = slice(c * CH, c * CH + width)
             nc.vector.tensor_tensor(
                 out=xp[j][:, cols], in0=xb[j][:, cols].bitcast(FP8), in1=sc[c][:, 0:width], op=MULT
+            )
+
+        def product_cols(j, c0, c1):
+            if j not in xp:
+                xp[j] = xp_pool.tile([P, K], BF16, name="xp")
+            c = c0 // CH
+            nc.vector.tensor_tensor(
+                out=xp[j][:, c0:c1],
+                in0=xb[j][:, c0:c1].bitcast(FP8),
+                in1=sc[c][:, c0 - c * CH : c1 - c * CH],
+                op=MULT,
             )
 
         def widen(j):
@@ -227,26 +257,28 @@ def tile_moelineara_kernel(tc, x_bytes, x_scale, W, *outs):
                 finish(j)
 
         with tc.manual_schedule():
-            load_scale(0)
+            load_scale()
             load_x(0, 0, 2048)
-            nc.sync.dma_start(out=sk[:], in_=sv[K - 512 : K].rearrange("(p t) -> p t", t=4))
-            load_scale(1)
             load_x(0, 2048, K)
-            load_scale(2)
-            load_scale(3)
             load_x(1)
             load_w(0)
             load_w(1)
             load_x(2)
             load_w(2)
             load_w(3)
+            nc.sync.dma_start(out=sk[:], in_=sv[K - 512 : K].rearrange("(p t) -> p t", t=4))
             for j in range(3, NT):
                 load_x(j)
 
-            widen(0)
-            for j in (0, 1):
-                half(j, 0)
-                half(j, 1)
+            turn_scale()
+            for b in range(8):
+                spread_scale(b)
+            for b in range(8):
+                for j in (0, 1):
+                    product_cols(j, 512 * b, 512 * (b + 1))
+                if b % 2 == 1:
+                    for j in (0, 1):
+                        turn_x(j, b // 4, (b // 2) % 2)
             for j in (0, 1):
                 quant_x(j, 0)
                 quant_x(j, 1)

@@ -23,7 +23,7 @@ NW = NE * R
 PASSES = 8
 CH = 1024
 GROUPS = ((0, 4), (4, 8), (8, 12), (12, 15), (15, 16))
-XT = (4, 5, 6, 7, 8, 10, 11, 12, 13, 14)
+XT = (3, 4, 5, 6, 7, 8, 9, 10, 11, 12, 13, 14, 15)
 
 
 def tile_moelineara_kernel(tc, x_bytes, x_scale, W, *outs):
@@ -102,6 +102,15 @@ def tile_moelineara_kernel(tc, x_bytes, x_scale, W, *outs):
             cols = slice(c * CH, c * CH + width)
             nc.vector.tensor_tensor(
                 out=xp[j][:, cols], in0=xb[j][:, cols].bitcast(FP8), in1=sc[c][:, 0:width], op=MULT
+            )
+
+        def spread_half(a):
+            tp = tp_pool.tile([P, 2, 2, P], F32, name="tp")
+            for i in range(2):
+                m = 2 * a + i
+                nc.tensor.transpose(tp[:, 0, i, :], scol[:, m : m + 1].to_broadcast([P, P]), ident[:])
+            nc.scalar.copy(
+                out=sc[0][:, 256 * a : 256 * (a + 1)], in_=tp[:, 0, :, :].rearrange("p u r -> p (u r)")
             )
 
         def product_cols(j, c0, c1):
@@ -259,8 +268,9 @@ def tile_moelineara_kernel(tc, x_bytes, x_scale, W, *outs):
         with tc.manual_schedule():
             load_scale()
             load_x(0, 0, 2048)
+            load_x(1, 0, 2048)
             load_x(0, 2048, K)
-            load_x(1)
+            load_x(1, 2048, K)
             load_w(0)
             load_w(1)
             load_x(2)
@@ -271,9 +281,14 @@ def tile_moelineara_kernel(tc, x_bytes, x_scale, W, *outs):
                 load_x(j)
 
             turn_scale()
-            for b in range(8):
+            for a in range(2):
+                spread_half(a)
+            for b in range(1, 8):
                 spread_scale(b)
-            for b in range(8):
+            for a in range(2):
+                for j in (0, 1):
+                    product_cols(j, 256 * a, 256 * (a + 1))
+            for b in range(1, 8):
                 for j in (0, 1):
                     product_cols(j, 512 * b, 512 * (b + 1))
                 if b % 2 == 1:

@@ -195,15 +195,16 @@ def tile_moelineara_kernel(tc, x_bytes, x_scale, W, *outs):
 
         def half(j, h):
             if h == 0:
-                scaled_turn(j)
                 scaled_out(j, 0)
+                widen(j + 1)
             else:
                 scaled_out(j, 1)
-                widen(j + 1)
             for b in range(2):
                 product(j, 2 * h + b)
             for b in range(2):
                 turn_x(j, h, b)
+            if h == 1:
+                scaled_turn(j + 1)
 
         def turn_w(g):
             words = wraw[g // 2][:].rearrange("p i k -> p (i k)").bitcast(F32)
@@ -321,7 +322,6 @@ def tile_moelineara_kernel(tc, x_bytes, x_scale, W, *outs):
                     half(j + 1, h)
                     quant_x(j, h)
                     passes(j, 4 * h, 4 * h + 4)
-            scaled_turn(15)
             scaled_out(15, 0)
             quant_x(14, 0)
             passes(14, 0, 4)

@@ -270,9 +270,9 @@ def tile_moelineara_kernel(tc, x_bytes, x_scale, W, *outs):
             load_scale()
             load_x(0, 0, 2048)
             load_x(1, 0, 2048)
+            load_w(0)
             load_x(0, 2048, K)
             load_x(1, 2048, K)
-            load_w(0)
             load_w(1)
             load_x(2)
             load_w(2)
@@ -295,29 +295,33 @@ def tile_moelineara_kernel(tc, x_bytes, x_scale, W, *outs):
                 if b % 2 == 1:
                     for j in (0, 1):
                         turn_x(j, b // 4, (b // 2) % 2)
-            for j in (0, 1):
-                quant_x(j, 0)
-                quant_x(j, 1)
-            for g in range(4):
-                turn_w(g)
-            half(2, 0)
-            half(2, 1)
-            for g in range(4):
+                    turn_w(b // 2)
+            product(2, 0)
+            product(2, 1)
+            quant_x(0, 0)
+            quant_x(0, 1)
+            quant_x(1, 0)
+            for g in range(3):
                 quant_w(g)
+            quant_x(1, 1)
+            quant_w(3)
             for g in range(4, 8):
                 turn_w(g)
             passes(0, 0, 4)
+            widen(3)
+            turn_x(2, 0, 0)
+            turn_x(2, 0, 1)
             passes(1, 0, 4)
-            half(3, 0)
-            half(3, 1)
-            quant_x(2, 0)
-            quant_x(2, 1)
             for g in range(4, 8):
                 quant_w(g)
             passes(0, 4, 8)
+            product(2, 2)
+            product(2, 3)
+            turn_x(2, 1, 0)
+            turn_x(2, 1, 1)
+            scaled_turn(3)
             passes(1, 4, 8)
-            passes(2, 0, 8)
-            for j in range(3, 14):
+            for j in range(2, 14):
                 for h in range(2):
                     half(j + 1, h)
                     quant_x(j, h)

@@ -24,6 +24,7 @@ PASSES = 8
 CH = 1024
 GROUPS = ((0, 4), (4, 8), (8, 12), (12, 15), (15, 16))
 XT = (3, 4, 5, 6, 7, 8, 9, 10, 11, 12, 13, 14, 15)
+XT2 = (4, 7, 10, 13)
 
 
 def tile_moelineara_kernel(tc, x_bytes, x_scale, W, *outs):
@@ -39,7 +40,7 @@ def tile_moelineara_kernel(tc, x_bytes, x_scale, W, *outs):
         xp_pool = ctx.enter_context(tc.tile_pool(name="xpp", bufs=3))
         grp_pool = ctx.enter_context(tc.tile_pool(name="grpp", bufs=8))
         xc_pool = ctx.enter_context(tc.tile_pool(name="xcp", bufs=4))
-        xq_pool = ctx.enter_context(tc.tile_pool(name="xqp", bufs=3))
+        xq_pool = ctx.enter_context(tc.tile_pool(name="xqp", bufs=4))
         res_pool = ctx.enter_context(tc.tile_pool(name="resp", bufs=2))
         tp_pool = ctx.enter_context(tc.psum_pool(name="tpp", bufs=6))
         acc_pool = ctx.enter_context(tc.psum_pool(name="accp", bufs=2))
@@ -53,7 +54,7 @@ def tile_moelineara_kernel(tc, x_bytes, x_scale, W, *outs):
         wraw = [const.tile([P, 4, CH], BF16, name="wraw%d" % c) for c in range(K // CH)]
         wc = [const.tile([P, NW], U32, name="wc%d" % g, align_bytes=64) for g in range(PASSES)]
         ws = [const.tile([P, NW], U8, name="ws%d" % g, align_bytes=64) for g in range(PASSES)]
-        sk = const.tile([P, 4], F32, name="sk")
+        sk = const.tile([P, 2, 4], F32, name="sk")
         srow = const.tile([P, P], F32, name="srow")
         scol = const.tile([P, K // P], F32, name="scol")
         xq = {}
@@ -99,6 +100,8 @@ def tile_moelineara_kernel(tc, x_bytes, x_scale, W, *outs):
             if j not in xp:
                 xp[j] = xp_pool.tile([P, K], BF16, name="xp")
             width = 512 if (c == 3 and j in XT) else CH
+            if c == 3 and j in XT2:
+                return
             cols = slice(c * CH, c * CH + width)
             nc.vector.tensor_tensor(
                 out=xp[j][:, cols], in0=xb[j][:, cols].bitcast(FP8), in1=sc[c][:, 0:width], op=MULT
@@ -124,35 +127,39 @@ def tile_moelineara_kernel(tc, x_bytes, x_scale, W, *outs):
                 op=MULT,
             )
 
-        def widen(j):
-            if j in XT:
-                xq[j] = xq_pool.tile([P, 512], BF16, name="xq")
-                nc.scalar.copy(out=xq[j][:], in_=xb[j][:, K - 512 : K].bitcast(FP8))
+        def on_road(j, g):
+            return (g == 7 and j in XT) or (g == 6 and j in XT2)
 
-        def scaled_turn(j):
-            if j not in XT:
+        def widen(j, g=7):
+            if on_road(j, g):
+                xq[(j, g)] = xq_pool.tile([P, 512], BF16, name="xq")
+                nc.scalar.copy(out=xq[(j, g)][:], in_=xb[j][:, 512 * g : 512 * (g + 1)].bitcast(FP8))
+
+        def scaled_turn(j, g=7):
+            if not on_road(j, g):
                 return
-            grp[("x", j, 1)] = grp_pool.tile([P, 2048], BF16, name="grp", align_bytes=64)
-            qwords = xq[j][:].bitcast(F32)
-            tpx[j] = tp_pool.tile([P, 2, 2, P], F32, name="tp")
+            if g == 7:
+                grp[("x", j, 1)] = grp_pool.tile([P, 2048], BF16, name="grp", align_bytes=64)
+            qwords = xq[(j, g)][:].bitcast(F32)
+            tpx[(j, g)] = tp_pool.tile([P, 2, 2, P], F32, name="tp")
             for u in range(2):
-                nc.tensor.transpose(tpx[j][:, 0, u, :], qwords[:, u:256:2], ident[:])
+                nc.tensor.transpose(tpx[(j, g)][:, 0, u, :], qwords[:, u:256:2], ident[:])
 
-        def scaled_out(j, u):
-            if j not in XT:
+        def scaled_out(j, u, g=7):
+            if not on_road(j, g):
                 return
             if u == 0:
-                planes[j] = xq_pool.tile([P, 4, P], BF16, name="planes")
-            pair = tpx[j][:, 0, u, :].bitcast(BF16).rearrange("p (r e) -> p r e", e=2)
+                planes[(j, g)] = xq_pool.tile([P, 4, P], BF16, name="planes")
+            pair = tpx[(j, g)][:, 0, u, :].bitcast(BF16).rearrange("p (r e) -> p r e", e=2)
             for e in range(2):
                 t = 2 * u + e
                 nc.scalar.activation(
-                    out=planes[j][:, t, :], in_=pair[:, :, e], func=COPY, scale=sk[:, t : t + 1]
+                    out=planes[(j, g)][:, t, :], in_=pair[:, :, e], func=COPY, scale=sk[:, g - 6, t : t + 1]
                 )
             if u == 1:
                 nc.scalar.copy(
-                    out=grp[("x", j, 1)][:, 1536:2048].rearrange("p (r t) -> p r t", t=4),
-                    in_=planes[j][:].rearrange("p t r -> p r t"),
+                    out=grp[("x", j, 1)][:, 512 * (g - 4) : 512 * (g - 3)].rearrange("p (r t) -> p r t", t=4),
+                    in_=planes[(j, g)][:].rearrange("p t r -> p r t"),
                 )
 
         def turn_last(j):
@@ -180,6 +187,9 @@ def tile_moelineara_kernel(tc, x_bytes, x_scale, W, *outs):
             )
 
         def turn_x(j, h, b):
+            if h == 1 and b == 1 and j in XT2:
+                scaled_turn(j, 6)
+                return
             if h == 1 and b == 1 and j in XT:
                 turn_last(j)
                 return
@@ -195,10 +205,13 @@ def tile_moelineara_kernel(tc, x_bytes, x_scale, W, *outs):
 
         def half(j, h):
             if h == 0:
+                scaled_out(j - 1, 0, 6)
+                scaled_out(j - 1, 1, 6)
                 scaled_out(j, 0)
                 widen(j + 1)
             else:
                 scaled_out(j, 1)
+                widen(j + 1, 6)
             for b in range(2):
                 product(j, 2 * h + b)
             for b in range(2):
@@ -277,7 +290,7 @@ def tile_moelineara_kernel(tc, x_bytes, x_scale, W, *outs):
             load_x(2)
             load_w(2)
             load_w(3)
-            nc.sync.dma_start(out=sk[:], in_=sv[K - 512 : K].rearrange("(p t) -> p t", t=4))
+            nc.sync.dma_start(out=sk[:], in_=sv[K - 1024 : K].rearrange("(g p t) -> p g t", g=2, t=4))
             for j in range(3, NT):
                 load_x(j)
 

@@ -24,7 +24,7 @@ PASSES = 8
 CH = 1024
 GROUPS = ((0, 4), (4, 8), (8, 12), (12, 15), (15, 16))
 XT = (3, 4, 5, 6, 7, 8, 9, 10, 11, 12, 13, 14, 15)
-XT2 = (4, 7, 10, 13)
+XT2 = (4, 8, 12)
 
 
 def tile_moelineara_kernel(tc, x_bytes, x_scale, W, *outs):

from contextlib import ExitStack

import concourse.mybir as mybir
from concourse.masks import make_identity

FLOPS = 2 * 2048 * 4096 * 512

F32 = mybir.dt.float32
BF16 = mybir.dt.bfloat16
U32 = mybir.dt.uint32
U8 = mybir.dt.uint8
FP8 = mybir.dt.float8_e4m3fn
FP8X4 = mybir.dt.float8_e4m3fn_x4
MULT = mybir.AluOpType.mult
COPY = mybir.ActivationFunctionType.Copy

P = 128
K = 4096
NT = 16
NE = 8
R = 64
NW = NE * R
PASSES = 8
CH = 1024
GROUPS = ((0, 4), (4, 8), (8, 12), (12, 15), (15, 16))
XT = (3, 4, 5, 6, 7, 8, 9, 10, 11, 12, 13, 14, 15)
XT2 = (4, 8, 12)


def tile_moelineara_kernel(tc, x_bytes, x_scale, W, *outs):
    nc = tc.nc
    xv = x_bytes.flatten_outer_dims().rearrange("(p j) k -> p j k", j=NT)
    sv = x_scale.rearrange("a b k -> (a b k)")
    wv = W.flatten_outer_dims().rearrange("(i p) k -> p i k", p=P)
    ov = [o.flatten_outer_dims().rearrange("(p j) r -> p j r", j=NT) for o in outs]

    with ExitStack() as ctx:
        const = ctx.enter_context(tc.tile_pool(name="const", bufs=1))
        xb_pool = ctx.enter_context(tc.tile_pool(name="xbp", bufs=NT))
        xp_pool = ctx.enter_context(tc.tile_pool(name="xpp", bufs=3))
        grp_pool = ctx.enter_context(tc.tile_pool(name="grpp", bufs=8))
        xc_pool = ctx.enter_context(tc.tile_pool(name="xcp", bufs=4))
        xq_pool = ctx.enter_context(tc.tile_pool(name="xqp", bufs=4))
        res_pool = ctx.enter_context(tc.tile_pool(name="resp", bufs=2))
        tp_pool = ctx.enter_context(tc.psum_pool(name="tpp", bufs=6))
        acc_pool = ctx.enter_context(tc.psum_pool(name="accp", bufs=2))

        ident = const.tile([P, P], F32, name="ident")
        make_identity(nc, ident[:])
        warm = const.tile([P, 1], F32, name="warm")
        nc.scalar.copy(out=warm[:], in_=ident[:, 0:1])

        sc = [const.tile([P, CH], F32, name="sc%d" % c) for c in range(K // CH)]
        wraw = [const.tile([P, 4, CH], BF16, name="wraw%d" % c) for c in range(K // CH)]
        wc = [const.tile([P, NW], U32, name="wc%d" % g, align_bytes=64) for g in range(PASSES)]
        ws = [const.tile([P, NW], U8, name="ws%d" % g, align_bytes=64) for g in range(PASSES)]
        sk = const.tile([P, 2, 4], F32, name="sk")
        srow = const.tile([P, P], F32, name="srow")
        scol = const.tile([P, K // P], F32, name="scol")
        xq = {}
        tpx = {}
        planes = {}
        xb = {}
        xp = {}
        grp = {}
        xc = {}
        xs = {}
        acc = {}
        res = {}

        def load_scale():
            nc.vector.memset(srow[32:64, :], 0.0)
            nc.vector.memset(srow[64:128, :], 0.0)
            nc.sync.dma_start(out=srow[0:32, :], in_=sv.rearrange("(m r) -> m r", r=P))

        def turn_scale():
            tp = tp_pool.tile([P, 2, 2, P], F32, name="tp")
            nc.tensor.transpose(tp[:, 0, 0, :], srow[:], ident[:])
            nc.scalar.copy(out=scol[:], in_=tp[:, 0, 0, 0 : K // P])

        def spread_scale(b):
            tp = tp_pool.tile([P, 2, 2, P], F32, name="tp")
            for i in range(4):
                m = 4 * b + i
                nc.tensor.transpose(tp[:, i // 2, i % 2, :], scol[:, m : m + 1].to_broadcast([P, P]), ident[:])
            nc.scalar.copy(
                out=sc[b // 2][:, 512 * (b % 2) : 512 * (b % 2 + 1)],
                in_=tp[:].rearrange("p a u r -> p (a u r)"),
            )

        def load_x(j, c0=0, c1=K):
            if j not in xb:
                xb[j] = xb_pool.tile([P, K], U8, name="xb")
            nc.sync.dma_start(out=xb[j][:, c0:c1], in_=xv[:, j, c0:c1])

        def load_w(c):
            nc.sync.dma_start(out=wraw[c][:], in_=wv[:, :, c * CH : (c + 1) * CH])

        def product(j, c):
            if j not in xp:
                xp[j] = xp_pool.tile([P, K], BF16, name="xp")
            width = 512 if (c == 3 and j in XT) else CH
            if c == 3 and j in XT2:
                return
            cols = slice(c * CH, c * CH + width)
            nc.vector.tensor_tensor(
                out=xp[j][:, cols], in0=xb[j][:, cols].bitcast(FP8), in1=sc[c][:, 0:width], op=MULT
            )

        def spread_half(a):
            tp = tp_pool.tile([P, 2, 2, P], F32, name="tp")
            for i in range(2):
                m = 2 * a + i
                nc.tensor.transpose(tp[:, 0, i, :], scol[:, m : m + 1].to_broadcast([P, P]), ident[:])
            nc.scalar.copy(
                out=sc[0][:, 256 * a : 256 * (a + 1)], in_=tp[:, 0, :, :].rearrange("p u r -> p (u r)")
            )

        def product_cols(j, c0, c1):
            if j not in xp:
                xp[j] = xp_pool.tile([P, K], BF16, name="xp")
            c = c0 // CH
            nc.vector.tensor_tensor(
                out=xp[j][:, c0:c1],
                in0=xb[j][:, c0:c1].bitcast(FP8),
                in1=sc[c][:, c0 - c * CH : c1 - c * CH],
                op=MULT,
            )

        def on_road(j, g):
            return (g == 7 and j in XT) or (g == 6 and j in XT2)

        def widen(j, g=7):
            if on_road(j, g):
                xq[(j, g)] = xq_pool.tile([P, 512], BF16, name="xq")
                nc.scalar.copy(out=xq[(j, g)][:], in_=xb[j][:, 512 * g : 512 * (g + 1)].bitcast(FP8))

        def scaled_turn(j, g=7):
            if not on_road(j, g):
                return
            if g == 7:
                grp[("x", j, 1)] = grp_pool.tile([P, 2048], BF16, name="grp", align_bytes=64)
            qwords = xq[(j, g)][:].bitcast(F32)
            tpx[(j, g)] = tp_pool.tile([P, 2, 2, P], F32, name="tp")
            for u in range(2):
                nc.tensor.transpose(tpx[(j, g)][:, 0, u, :], qwords[:, u:256:2], ident[:])

        def scaled_out(j, u, g=7):
            if not on_road(j, g):
                return
            if u == 0:
                planes[(j, g)] = xq_pool.tile([P, 4, P], BF16, name="planes")
            pair = tpx[(j, g)][:, 0, u, :].bitcast(BF16).rearrange("p (r e) -> p r e", e=2)
            for e in range(2):
                t = 2 * u + e
                nc.scalar.activation(
                    out=planes[(j, g)][:, t, :], in_=pair[:, :, e], func=COPY, scale=sk[:, g - 6, t : t + 1]
                )
            if u == 1:
                nc.scalar.copy(
                    out=grp[("x", j, 1)][:, 512 * (g - 4) : 512 * (g - 3)].rearrange("p (r t) -> p r t", t=4),
                    in_=planes[(j, g)][:].rearrange("p t r -> p r t"),
                )

        def turn_last(j):
            gw = grp[("x", j, 1)][:].bitcast(F32)
            words = xp[j][:].bitcast(F32)
            tp = tp_pool.tile([P, 2, 2, P], F32, name="tp")
            for u in range(2):
                nc.tensor.transpose(tp[:, 0, u, :], words[:, 256 * 6 + u : 256 * 7 : 2], ident[:])
            nc.scalar.copy(
                out=gw[:, 512:768].rearrange("p (r u) -> p r u", u=2),
                in_=tp[:, 0, :, :].rearrange("p u r -> p r u"),
            )

        def bank(key, b, slices):
            if key not in grp:
                grp[key] = grp_pool.tile([P, 2048], BF16, name="grp", align_bytes=64)
            gw = grp[key][:].bitcast(F32)
            tp = tp_pool.tile([P, 2, 2, P], F32, name="tp")
            for a in range(2):
                for u in range(2):
                    nc.tensor.transpose(tp[:, a, u, :], slices[a][u], ident[:])
            nc.scalar.copy(
                out=gw[:, 512 * b : 512 * (b + 1)].rearrange("p (a r u) -> p a r u", a=2, u=2),
                in_=tp[:].rearrange("p a u r -> p a r u"),
            )

        def turn_x(j, h, b):
            if h == 1 and b == 1 and j in XT2:
                scaled_turn(j, 6)
                return
            if h == 1 and b == 1 and j in XT:
                turn_last(j)
                return
            words = xp[j][:].bitcast(F32)
            bank(
                ("x", j, h),
                b,
                [
                    [words[:, 256 * g + u : 256 * (g + 1) : 2] for u in range(2)]
                    for g in (4 * h + 2 * b, 4 * h + 2 * b + 1)
                ],
            )

        def half(j, h):
            if h == 0:
                scaled_out(j - 1, 0, 6)
                scaled_out(j - 1, 1, 6)
                scaled_out(j, 0)
                widen(j + 1)
            else:
                scaled_out(j, 1)
                widen(j + 1, 6)
            for b in range(2):
                product(j, 2 * h + b)
            for b in range(2):
                turn_x(j, h, b)
            if h == 1:
                scaled_turn(j + 1)

        def turn_w(g):
            words = wraw[g // 2][:].rearrange("p i k -> p (i k)").bitcast(F32)
            gl = g % 2
            for b in range(2):
                bank(
                    ("w", g),
                    b,
                    [
                        [
                            words[:, 512 * i + 256 * gl + u : 512 * i + 256 * (gl + 1) : 2]
                            for u in range(2)
                        ]
                        for i in (2 * b, 2 * b + 1)
                    ],
                )

        def quant_x(j, h, b0=0, b1=2):
            if j not in xc:
                xc[j] = xc_pool.tile([P, 1024], U32, name="xc", align_bytes=64)
                xs[j] = xc_pool.tile([P, 1024], U8, name="xs", align_bytes=64)
            cols = slice(512 * h + 256 * b0, 512 * h + 256 * b1)
            nc.vector.quantize_mx(
                out=xc[j][:, cols].bitcast(FP8X4),
                scales=xs[j][:, cols],
                in_=grp[("x", j, h)][:, 1024 * b0 : 1024 * b1],
            )

        def quant_w(g):
            nc.vector.quantize_mx(out=wc[g][:].bitcast(FP8X4), scales=ws[g][:], in_=grp[("w", g)][:])

        def finish(j):
            for j0, j1 in GROUPS:
                if j0 <= j < j1:
                    if j == j0:
                        res[j0] = res_pool.tile([P, NE, j1 - j0, R], F32, name="res")
                    nc.scalar.copy(
                        out=res[j0][:, :, j - j0, :],
                        in_=acc[j][:].rearrange("p (e r) -> p e r", e=NE),
                    )
                    if j == j1 - 1:
                        for e in range(NE):
                            nc.sync.dma_start(out=ov[e][:, j0:j1, :], in_=res[j0][:, e, :, :])

        def passes(j, g0, g1):
            if g0 == 0:
                acc[j] = acc_pool.tile([P, NW], F32, name="acc")
            for g in range(g0, g1):
                cols = slice(P * g, P * (g + 1))
                nc.tensor.matmul_mx(
                    out=acc[j][:],
                    lhsT=xc[j][:, cols].bitcast(FP8X4),
                    lhsT_scale=xs[j][:, cols],
                    rhs=wc[g][:].bitcast(FP8X4),
                    rhs_scale=ws[g][:],
                    start=(g == 0),
                    stop=(g == PASSES - 1),
                )
            if g1 == PASSES:
                finish(j)

        with tc.manual_schedule():
            load_scale()
            load_x(0, 0, 2048)
            load_x(1, 0, 2048)
            load_w(0)
            load_x(0, 2048, K)
            load_x(1, 2048, K)
            load_w(1)
            load_x(2)
            load_w(2)
            load_w(3)
            nc.sync.dma_start(out=sk[:], in_=sv[K - 1024 : K].rearrange("(g p t) -> p g t", g=2, t=4))
            for j in range(3, NT):
                load_x(j)

            turn_scale()
            for a in range(2):
                spread_half(a)
            for b in range(1, 8):
                spread_scale(b)
            for a in range(2):
                for j in (0, 1):
                    product_cols(j, 256 * a, 256 * (a + 1))
            for b in range(1, 8):
                for j in (0, 1):
                    product_cols(j, 512 * b, 512 * (b + 1))
                if b % 2 == 1:
                    for j in (0, 1):
                        turn_x(j, b // 4, (b // 2) % 2)
                    turn_w(b // 2)
            product(2, 0)
            product(2, 1)
            quant_x(0, 0)
            quant_x(0, 1)
            quant_x(1, 0)
            for g in range(3):
                quant_w(g)
            quant_x(1, 1)
            quant_w(3)
            for g in range(4, 8):
                turn_w(g)
            passes(0, 0, 4)
            widen(3)
            turn_x(2, 0, 0)
            turn_x(2, 0, 1)
            passes(1, 0, 4)
            for g in range(4, 8):
                quant_w(g)
            passes(0, 4, 8)
            product(2, 2)
            product(2, 3)
            turn_x(2, 1, 0)
            turn_x(2, 1, 1)
            scaled_turn(3)
            passes(1, 4, 8)
            for j in range(2, 14):
                for h in range(2):
                    half(j + 1, h)
                    quant_x(j, h)
                    passes(j, 4 * h, 4 * h + 4)
            scaled_out(15, 0)
            quant_x(14, 0)
            passes(14, 0, 4)
            product(15, 0)
            turn_x(15, 0, 0)
            scaled_out(15, 1)
            quant_x(14, 1)
            passes(14, 4, 8)
            product(15, 1)
            turn_x(15, 0, 1)
            product(15, 2)
            turn_x(15, 1, 0)
            quant_x(15, 0, 0, 1)
            passes(15, 0, 2)
            product(15, 3)
            turn_x(15, 1, 1)
            quant_x(15, 0, 1, 2)
            passes(15, 2, 4)
            quant_x(15, 1, 0, 1)
            passes(15, 4, 6)
            quant_x(15, 1, 1, 2)
            passes(15, 6, 8)
